import numpy as np
import ml_dtypes


def mxq(x, axis, fmt="e4m3"):
    dtype, down = {"e4m3": (ml_dtypes.float8_e4m3fn, 7), "e5m2": (ml_dtypes.float8_e5m2, 14)}[fmt]
    v = np.moveaxis(np.asarray(x, np.float32).astype(ml_dtypes.bfloat16).astype(np.float64), axis, -1)
    blocks = v.reshape(v.shape[:-1] + (-1, 32))
    amax = np.abs(blocks).max(-1, keepdims=True)
    byte = np.maximum(np.where(amax > 0, np.frexp(amax)[1] - 1 + 127, 0) - down, 1)
    scale = np.exp2(byte - 127.0)
    codes = (blocks / scale).astype(np.float32).astype(dtype).astype(np.float64)
    return np.moveaxis((codes * scale).reshape(v.shape), -1, axis)


WIDE = False


def mx_kscale(k):
    if not WIDE:
        return np.ones(k)
    levels = np.array([10, -10, 5, -5, 0])
    a = np.random.permutation(np.resize(levels, k // 512 * 4)).reshape(k // 512, 4)
    idx = np.arange(k)
    return np.exp2(a[idx // 512, idx % 128 // 32])


BF16 = ml_dtypes.bfloat16


def bf(x):
    return np.asarray(x, np.float32).astype(BF16)


def f64(x):
    return np.asarray(x).astype(np.float64)


B, S, DIM, QK, EXP, V, G = 1, 1024, 1024, 128, 2048, 1024, 512
W = 2 * QK + 2 * EXP
EPS = 1e-5
ERF_TERMS = 100


def erf(z):
    a = np.minimum(np.abs(z), 6.0)
    a2 = 2.0 * a * a
    term = a.copy()
    tot = a.copy()
    for n in range(1, ERF_TERMS):
        term *= a2
        term /= 2 * n + 1
        tot += term
    return np.sign(z) * 2.0 / np.sqrt(np.pi) * np.exp(-a * a) * tot


def gelu_erf(v):
    return 0.5 * v * (1.0 + erf(v / np.sqrt(2.0)))


def setup_inputs():
    s = mx_kscale(DIM)
    rows = np.exp2(np.random.uniform(-8.0, 1.0, (B, S, 1)))
    off = 0.5 * np.random.standard_normal((B, S, 1))
    gain = np.where(np.arange(W) < 2 * QK, 1.5, 1.0)[:, None]
    return {"x": bf((np.random.standard_normal((B, S, DIM)) + off) * rows),
            "norm_w": bf((1.0 + 0.1 * np.random.standard_normal(DIM)) * s),
            "expand_w": bf(np.random.standard_normal((W, DIM)) * gain / np.sqrt(DIM) / s)}


def reference(x, norm_w, expand_w):
    x = f64(x)
    mu = x.mean(-1, keepdims=True)
    var = ((x - mu) ** 2).mean(-1, keepdims=True)
    h = (x - mu) * (1.0 / np.sqrt(var + EPS)) * f64(norm_w)
    proj = mxq(h, 2, "e4m3") @ mxq(f64(expand_w), 1, "e4m3").T
    q = proj[..., :QK]
    k = proj[..., QK:2 * QK]
    lin = proj[..., 2 * QK:2 * QK + EXP]
    pre = proj[..., 2 * QK + EXP:]
    geglu = lin * gelu_erf(pre)
    return q, k, geglu[..., :EXP - V], geglu[..., EXP - V:]

@@ -1,0 +1,198 @@
+from contextlib import ExitStack
+
+import concourse.mybir as mybir
+from concourse.masks import make_identity
+
+F32 = mybir.dt.float32
+BF16 = mybir.dt.bfloat16
+U32 = mybir.dt.uint32
+U8 = mybir.dt.uint8
+FP8X4 = mybir.dt.float8_e4m3fn_x4
+ACT = mybir.ActivationFunctionType
+ALU = mybir.AluOpType
+
+P = 128
+TOKENS = 1024
+DIM = 1024
+QK = 128
+EXP = 2048
+W_ROWS = 2 * QK + 2 * EXP
+EPS = 1e-5
+
+PACK = 4
+K_PASS = P * PACK
+PASSES = DIM // K_PASS
+TOKEN_TILES = TOKENS // P
+TILES_PER_LOAD = 2
+GROUP_ROWS = 2 * P
+GROUPS = W_ROWS // GROUP_ROWS
+N_TILE = 512
+UNITS = EXP // N_TILE
+BN_CHUNK = 512
+
+FLOPS = 2 * TOKENS * DIM * W_ROWS
+
+
+def tile_latentattentionblock_pa_kernel(tc, x, norm_w, expand_w, q_out, k_out, gl_out, gv_out):
+    nc = tc.nc
+    x_view = x.rearrange("b (p m) k -> p (b m) k", m=TOKEN_TILES)
+    q_view = q_out.rearrange("b (p m) c -> p (b m) c", m=TOKEN_TILES)
+    k_view = k_out.rearrange("b (p m) c -> p (b m) c", m=TOKEN_TILES)
+    g_views = [
+        gl_out.rearrange("b (p m) c -> p (b m) c", m=TOKEN_TILES),
+        gv_out.rearrange("b (p m) c -> p (b m) c", m=TOKEN_TILES),
+    ]
+
+    with ExitStack() as ctx:
+        const = ctx.enter_context(tc.tile_pool(name="const", bufs=1))
+        x_pool = ctx.enter_context(tc.tile_pool(name="x_pool", bufs=TOKEN_TILES // TILES_PER_LOAD))
+        w_pool = ctx.enter_context(tc.tile_pool(name="w_pool", bufs=GROUPS))
+        small = ctx.enter_context(tc.tile_pool(name="small", bufs=4))
+        y_pool = ctx.enter_context(tc.tile_pool(name="y_pool", bufs=3))
+        grouped_pool = ctx.enter_context(tc.tile_pool(name="grouped_pool", bufs=4))
+        out_pool = ctx.enter_context(tc.tile_pool(name="out_pool", bufs=4))
+        tp_psum = ctx.enter_context(tc.psum_pool(name="tp_psum", bufs=4))
+        mx_psum = ctx.enter_context(tc.psum_pool(name="mx_psum", bufs=2))
+
+        h_codes = const.tile([P, TOKEN_TILES, PASSES, P], U32, align_bytes=64)
+        h_scales = const.tile([P, TOKEN_TILES, PASSES, P], U8, align_bytes=64)
+        w_codes = const.tile([P, PASSES, W_ROWS], U32, align_bytes=64)
+        w_scales = const.tile([P, PASSES, W_ROWS], U8, align_bytes=64)
+        qk_sb = const.tile([P, 2, TOKEN_TILES, QK], F32)
+
+        group_order = []
+        for j in range(UNITS):
+            group_order.extend([1 + 2 * j, 2 + 2 * j, 9 + 2 * j, 10 + 2 * j])
+        group_order.append(0)
+
+        nw_rows = const.tile([P, 2 * P], BF16)
+        nc.vector.memset(nw_rows[:], 0.0)
+        nc.scalar.dma_start(out=nw_rows[0:PACK, :], in_=norm_w.rearrange("(c w) -> c w", w=2 * P))
+        x_raw = []
+        w_raw = {}
+        for c in range(TOKEN_TILES // TILES_PER_LOAD):
+            x_chunk = x_pool.tile([P, TILES_PER_LOAD, DIM], BF16)
+            nc.sync.dma_start(out=x_chunk[:], in_=x_view[:, TILES_PER_LOAD * c : TILES_PER_LOAD * (c + 1), :])
+            x_raw.append(x_chunk)
+            for w in group_order[4 * c : 4 * c + 4] + (group_order[16:] if c == 3 else []):
+                w_chunk = w_pool.tile([P, 2, DIM], BF16)
+                nc.sync.dma_start(
+                    out=w_chunk[:],
+                    in_=expand_w[GROUP_ROWS * w : GROUP_ROWS * (w + 1), :].rearrange("(p t) k -> p t k", t=2),
+                )
+                w_raw[w] = w_chunk
+
+        ident = const.tile([P, P], F32)
+        make_identity(nc, ident[:])
+        minus_half = const.tile([P, 1], F32)
+        nc.vector.memset(minus_half[:], -0.5)
+
+        nw_ps = tp_psum.tile([P, P], F32, tag="tp")
+        nc.tensor.transpose(nw_ps[:], nw_rows[:].bitcast(F32), ident[:])
+        nw_cols = const.tile([P, PASSES * PACK], F32)
+        nc.vector.tensor_copy(out=nw_cols[:], in_=nw_ps[:, 0:PACK].bitcast(BF16))
+
+        def layer_norm(m):
+            x_tile = x_raw[m // TILES_PER_LOAD][:, m % TILES_PER_LOAD, :]
+            stats = small.tile([P, DIM // BN_CHUNK, 6], F32)
+            for c in range(DIM // BN_CHUNK):
+                nc.vector.bn_stats(out=stats[:, c, :], in_=x_tile[:, BN_CHUNK * c : BN_CHUNK * (c + 1)])
+            mean_var = small.tile([P, 2], F32)
+            nc.vector.bn_aggr(out=mean_var[:], in_=stats[:].rearrange("p c s -> p (c s)"))
+            var_eps = small.tile([P, 1], F32)
+            nc.gpsimd.tensor_scalar(out=var_eps[:], in0=mean_var[:, 1:2], scalar1=EPS, scalar2=None, op0=ALU.add)
+            rstd = small.tile([P, 1], F32)
+            nc.gpsimd.tensor_tensor(out=rstd[:], in0=var_eps[:], in1=minus_half[:], op=ALU.pow)
+            shift = small.tile([P, 1], F32)
+            nc.gpsimd.tensor_scalar(
+                out=shift[:], in0=mean_var[:, 0:1], scalar1=rstd[:, 0:1], scalar2=-1.0, op0=ALU.mult, op1=ALU.mult
+            )
+            y = y_pool.tile([P, 2, DIM // 2], F32)
+            nc.scalar.activation(
+                out=y[:],
+                in_=x_tile.rearrange("p (j e) -> p e j", e=2),
+                func=ACT.Identity,
+                bias=shift[:, 0:1],
+                scale=rstd[:, 0:1],
+            )
+            h_grouped = grouped_pool.tile([P, PASSES, P, PACK], BF16, align_bytes=64)
+            for g in range(PASSES):
+                yt = tp_psum.tile([P, PACK, P], F32, tag="tp")
+                for u in range(2):
+                    for e in range(2):
+                        first = 2 * P * g + P * u
+                        nc.tensor.transpose(yt[:, 2 * u + e, :], y[:, e, first : first + P], ident[:])
+                nc.vector.tensor_tensor(
+                    out=h_grouped[:, g, :, :],
+                    in0=yt[:].rearrange("p t r -> p r t"),
+                    in1=nw_cols[:, PACK * g : PACK * (g + 1)].unsqueeze(1).to_broadcast([P, P, PACK]),
+                    op=ALU.mult,
+                )
+            nc.vector.quantize_mx(
+                out=h_codes[:, m, :, :].rearrange("p g r -> p (g r)").bitcast(FP8X4),
+                scales=h_scales[:, m, :, :].rearrange("p g r -> p (g r)"),
+                in_=h_grouped[:].rearrange("p g r t -> p (g r t)"),
+            )
+
+        def weight_group(w):
+            words = w_raw[w][:].bitcast(F32)
+            cols = slice(GROUP_ROWS * w, GROUP_ROWS * (w + 1))
+            w_grouped = grouped_pool.tile([P, PASSES, GROUP_ROWS * PACK], BF16, align_bytes=64)
+            for g in range(PASSES):
+                wt = tp_psum.tile([P, 2, 2, P], F32, tag="tp")
+                for t in range(2):
+                    for u in range(2):
+                        first = 2 * P * g + P * u
+                        nc.tensor.transpose(wt[:, t, u, :], words[:, t, first : first + P], ident[:])
+                nc.scalar.copy(
+                    out=w_grouped[:, g, :].bitcast(F32).rearrange("p (r t u) -> p r t u", t=2, u=2),
+                    in_=wt[:].rearrange("p t u r -> p r t u"),
+                )
+            for g in range(PASSES):
+                nc.vector.quantize_mx(
+                    out=w_codes[:, g, cols].bitcast(FP8X4), scales=w_scales[:, g, cols], in_=w_grouped[:, g, :]
+                )
+
+        def project(acc, m, first, width):
+            for g in range(PASSES):
+                nc.tensor.matmul_mx(
+                    out=acc,
+                    lhsT=h_codes[:, m, g, :].bitcast(FP8X4),
+                    lhsT_scale=h_scales[:, m, g, :],
+                    rhs=w_codes[:, g, first : first + width].bitcast(FP8X4),
+                    rhs_scale=w_scales[:, g, first : first + width],
+                    start=(g == 0),
+                    stop=(g == PASSES - 1),
+                )
+
+        def geglu(j, m):
+            lin = mx_psum.tile([P, N_TILE], F32)
+            pre = mx_psum.tile([P, N_TILE], F32)
+            project(pre[:], m, 2 * QK + EXP + N_TILE * j, N_TILE)
+            project(lin[:], m, 2 * QK + N_TILE * j, N_TILE)
+            gelu = out_pool.tile([P, N_TILE], F32)
+            nc.scalar.activation(out=gelu[:], in_=pre[:], func=ACT.Gelu)
+            prod = out_pool.tile([P, N_TILE], F32)
+            nc.vector.tensor_tensor(out=prod[:], in0=lin[:], in1=gelu[:], op=ALU.mult)
+            first = N_TILE * (j % 2)
+            nc.sync.dma_start(out=g_views[j // 2][:, m, first : first + N_TILE], in_=prod[:])
+
+        def q_and_k(m):
+            qk = mx_psum.tile([P, 2, QK], F32, tag="lin")
+            project(qk[:].rearrange("p a c -> p (a c)"), m, 0, 2 * QK)
+            nc.scalar.copy(out=qk_sb[:, :, m, :], in_=qk[:])
+
+        for c in range(TOKEN_TILES // TILES_PER_LOAD):
+            for m in range(TILES_PER_LOAD * c, TILES_PER_LOAD * (c + 1)):
+                layer_norm(m)
+            for w in group_order[4 * c : 4 * c + 4]:
+                weight_group(w)
+        weight_group(group_order[16])
+
+        for j in range(UNITS):
+            for m in range(TOKEN_TILES):
+                geglu(j, m)
+        for m in range(TOKEN_TILES):
+            q_and_k(m)
+        nc.sync.dma_start(out=q_view, in_=qk_sb[:, 0, :, :])
+        nc.sync.dma_start(out=k_view, in_=qk_sb[:, 1, :, :])

@@ -23,12 +23,15 @@ PACK = 4
 K_PASS = P * PACK
 PASSES = DIM // K_PASS
 TOKEN_TILES = TOKENS // P
-TILES_PER_LOAD = 2
 GROUP_ROWS = 2 * P
 GROUPS = W_ROWS // GROUP_ROWS
 N_TILE = 512
 UNITS = EXP // N_TILE
+GROUPS_PER_UNIT = 2 * N_TILE // GROUP_ROWS
+GROUPS_PER_TOKEN_TILE = (GROUPS - 1) // TOKEN_TILES
 BN_CHUNK = 512
+PSUM_BANKS = 8
+AHEAD = 2
 
 FLOPS = 2 * TOKENS * DIM * W_ROWS
 
@@ -44,15 +47,16 @@ def tile_latentattentionblock_pa_kernel(tc, x, norm_w, expand_w, q_out, k_out, g
     ]
 
     with ExitStack() as ctx:
+        ctx.enter_context(tc.manual_schedule())
         const = ctx.enter_context(tc.tile_pool(name="const", bufs=1))
-        x_pool = ctx.enter_context(tc.tile_pool(name="x_pool", bufs=TOKEN_TILES // TILES_PER_LOAD))
-        w_pool = ctx.enter_context(tc.tile_pool(name="w_pool", bufs=GROUPS))
+        x_pool = ctx.enter_context(tc.tile_pool(name="x_pool", bufs=TOKEN_TILES))
+        w_pool = ctx.enter_context(tc.tile_pool(name="w_pool", bufs=8))
         small = ctx.enter_context(tc.tile_pool(name="small", bufs=4))
-        y_pool = ctx.enter_context(tc.tile_pool(name="y_pool", bufs=3))
-        grouped_pool = ctx.enter_context(tc.tile_pool(name="grouped_pool", bufs=4))
+        y_pool = ctx.enter_context(tc.tile_pool(name="y_pool", bufs=AHEAD + 1))
+        h_pool = ctx.enter_context(tc.tile_pool(name="h_pool", bufs=3))
+        wg_pool = ctx.enter_context(tc.tile_pool(name="wg_pool", bufs=GROUPS))
         out_pool = ctx.enter_context(tc.tile_pool(name="out_pool", bufs=4))
-        tp_psum = ctx.enter_context(tc.psum_pool(name="tp_psum", bufs=4))
-        mx_psum = ctx.enter_context(tc.psum_pool(name="mx_psum", bufs=2))
+        psum = ctx.enter_context(tc.psum_pool(name="psum", bufs=PSUM_BANKS))
 
         h_codes = const.tile([P, TOKEN_TILES, PASSES, P], U32, align_bytes=64)
         h_scales = const.tile([P, TOKEN_TILES, PASSES, P], U8, align_bytes=64)
@@ -60,64 +64,88 @@ def tile_latentattentionblock_pa_kernel(tc, x, norm_w, expand_w, q_out, k_out, g
         w_scales = const.tile([P, PASSES, W_ROWS], U8, align_bytes=64)
         qk_sb = const.tile([P, 2, TOKEN_TILES, QK], F32)
 
-        group_order = []
+        first_lin = 1
+        first_pre = 1 + EXP // GROUP_ROWS
+        group_order = [0]
         for j in range(UNITS):
-            group_order.extend([1 + 2 * j, 2 + 2 * j, 9 + 2 * j, 10 + 2 * j])
-        group_order.append(0)
+            group_order.extend([first_pre + 2 * j, first_pre + 2 * j + 1, first_lin + 2 * j, first_lin + 2 * j + 1])
+
+        def groups_beside(m):
+            return group_order[GROUPS_PER_TOKEN_TILE * m : GROUPS_PER_TOKEN_TILE * (m + 1)]
+
+        groups_after = group_order[GROUPS_PER_TOKEN_TILE * TOKEN_TILES :]
 
         nw_rows = const.tile([P, 2 * P], BF16)
         nc.vector.memset(nw_rows[:], 0.0)
         nc.scalar.dma_start(out=nw_rows[0:PACK, :], in_=norm_w.rearrange("(c w) -> c w", w=2 * P))
-        x_raw = []
-        w_raw = {}
-        for c in range(TOKEN_TILES // TILES_PER_LOAD):
-            x_chunk = x_pool.tile([P, TILES_PER_LOAD, DIM], BF16)
-            nc.sync.dma_start(out=x_chunk[:], in_=x_view[:, TILES_PER_LOAD * c : TILES_PER_LOAD * (c + 1), :])
-            x_raw.append(x_chunk)
-            for w in group_order[4 * c : 4 * c + 4] + (group_order[16:] if c == 3 else []):
-                w_chunk = w_pool.tile([P, 2, DIM], BF16)
-                nc.sync.dma_start(
-                    out=w_chunk[:],
-                    in_=expand_w[GROUP_ROWS * w : GROUP_ROWS * (w + 1), :].rearrange("(p t) k -> p t k", t=2),
-                )
-                w_raw[w] = w_chunk
-
-        ident = const.tile([P, P], F32)
-        make_identity(nc, ident[:])
         minus_half = const.tile([P, 1], F32)
         nc.vector.memset(minus_half[:], -0.5)
+        ident = const.tile([P, P], F32)
+        make_identity(nc, ident[:])
+        table_warmer = const.tile([P, 1], F32)
+        nc.scalar.activation(out=table_warmer[:], in_=minus_half[:], func=ACT.Gelu)
 
-        nw_ps = tp_psum.tile([P, P], F32, tag="tp")
+        x_raw = {}
+        w_raw = {}
+
+        def load_tokens(m):
+            x_tile = x_pool.tile([P, DIM], BF16)
+            nc.sync.dma_start(out=x_tile[:], in_=x_view[:, m, :])
+            x_raw[m] = x_tile
+
+        def load_weights(w):
+            w_chunk = w_pool.tile([P, 2, DIM], BF16)
+            nc.sync.dma_start(
+                out=w_chunk[:],
+                in_=expand_w[GROUP_ROWS * w : GROUP_ROWS * (w + 1), :].rearrange("(p t) k -> p t k", t=2),
+            )
+            w_raw[w] = w_chunk
+
+        for m in range(AHEAD):
+            load_tokens(m)
+        for m in range(TOKEN_TILES):
+            for w in groups_beside(m):
+                load_weights(w)
+            if m + AHEAD < TOKEN_TILES:
+                load_tokens(m + AHEAD)
+        for w in groups_after:
+            load_weights(w)
+
+        nw_ps = psum.tile([P, P], F32, tag="bank")
         nc.tensor.transpose(nw_ps[:], nw_rows[:].bitcast(F32), ident[:])
         nw_cols = const.tile([P, PASSES * PACK], F32)
         nc.vector.tensor_copy(out=nw_cols[:], in_=nw_ps[:, 0:PACK].bitcast(BF16))
 
-        def layer_norm(m):
-            x_tile = x_raw[m // TILES_PER_LOAD][:, m % TILES_PER_LOAD, :]
+        y_tiles = {}
+        h_grouped_tiles = {}
+        w_grouped_tiles = {}
+
+        def normalise(m):
             stats = small.tile([P, DIM // BN_CHUNK, 6], F32)
             for c in range(DIM // BN_CHUNK):
-                nc.vector.bn_stats(out=stats[:, c, :], in_=x_tile[:, BN_CHUNK * c : BN_CHUNK * (c + 1)])
+                nc.vector.bn_stats(out=stats[:, c, :], in_=x_raw[m][:, BN_CHUNK * c : BN_CHUNK * (c + 1)])
             mean_var = small.tile([P, 2], F32)
             nc.vector.bn_aggr(out=mean_var[:], in_=stats[:].rearrange("p c s -> p (c s)"))
             var_eps = small.tile([P, 1], F32)
             nc.gpsimd.tensor_scalar(out=var_eps[:], in0=mean_var[:, 1:2], scalar1=EPS, scalar2=None, op0=ALU.add)
             rstd = small.tile([P, 1], F32)
             nc.gpsimd.tensor_tensor(out=rstd[:], in0=var_eps[:], in1=minus_half[:], op=ALU.pow)
-            shift = small.tile([P, 1], F32)
-            nc.gpsimd.tensor_scalar(
-                out=shift[:], in0=mean_var[:, 0:1], scalar1=rstd[:, 0:1], scalar2=-1.0, op0=ALU.mult, op1=ALU.mult
-            )
             y = y_pool.tile([P, 2, DIM // 2], F32)
-            nc.scalar.activation(
+            nc.gpsimd.tensor_scalar(
                 out=y[:],
-                in_=x_tile.rearrange("p (j e) -> p e j", e=2),
-                func=ACT.Identity,
-                bias=shift[:, 0:1],
-                scale=rstd[:, 0:1],
+                in0=x_raw[m][:].rearrange("p (j e) -> p e j", e=2),
+                scalar1=mean_var[:, 0:1],
+                scalar2=rstd[:, 0:1],
+                op0=ALU.subtract,
+                op1=ALU.mult,
             )
-            h_grouped = grouped_pool.tile([P, PASSES, P, PACK], BF16, align_bytes=64)
+            y_tiles[m] = y
+
+        def transpose_tokens(m):
+            y = y_tiles[m]
+            h_grouped = h_pool.tile([P, PASSES, P, PACK], BF16, align_bytes=64)
             for g in range(PASSES):
-                yt = tp_psum.tile([P, PACK, P], F32, tag="tp")
+                yt = psum.tile([P, PACK, P], F32, tag="bank")
                 for u in range(2):
                     for e in range(2):
                         first = 2 * P * g + P * u
@@ -128,18 +156,20 @@ def tile_latentattentionblock_pa_kernel(tc, x, norm_w, expand_w, q_out, k_out, g
                     in1=nw_cols[:, PACK * g : PACK * (g + 1)].unsqueeze(1).to_broadcast([P, P, PACK]),
                     op=ALU.mult,
                 )
+            h_grouped_tiles[m] = h_grouped
+
+        def quantise_tokens(m):
             nc.vector.quantize_mx(
                 out=h_codes[:, m, :, :].rearrange("p g r -> p (g r)").bitcast(FP8X4),
                 scales=h_scales[:, m, :, :].rearrange("p g r -> p (g r)"),
-                in_=h_grouped[:].rearrange("p g r t -> p (g r t)"),
+                in_=h_grouped_tiles[m][:].rearrange("p g r t -> p (g r t)"),
             )
 
-        def weight_group(w):
+        def transpose_weights(w):
             words = w_raw[w][:].bitcast(F32)
-            cols = slice(GROUP_ROWS * w, GROUP_ROWS * (w + 1))
-            w_grouped = grouped_pool.tile([P, PASSES, GROUP_ROWS * PACK], BF16, align_bytes=64)
+            w_grouped = wg_pool.tile([P, PASSES, GROUP_ROWS * PACK], BF16, align_bytes=64)
             for g in range(PASSES):
-                wt = tp_psum.tile([P, 2, 2, P], F32, tag="tp")
+                wt = psum.tile([P, 2, 2, P], F32, tag="bank")
                 for t in range(2):
                     for u in range(2):
                         first = 2 * P * g + P * u
@@ -148,9 +178,15 @@ def tile_latentattentionblock_pa_kernel(tc, x, norm_w, expand_w, q_out, k_out, g
                     out=w_grouped[:, g, :].bitcast(F32).rearrange("p (r t u) -> p r t u", t=2, u=2),
                     in_=wt[:].rearrange("p t u r -> p r t u"),
                 )
+            w_grouped_tiles[w] = w_grouped
+
+        def quantise_weights(w):
+            cols = slice(GROUP_ROWS * w, GROUP_ROWS * (w + 1))
             for g in range(PASSES):
                 nc.vector.quantize_mx(
-                    out=w_codes[:, g, cols].bitcast(FP8X4), scales=w_scales[:, g, cols], in_=w_grouped[:, g, :]
+                    out=w_codes[:, g, cols].bitcast(FP8X4),
+                    scales=w_scales[:, g, cols],
+                    in_=w_grouped_tiles[w][:, g, :],
                 )
 
         def project(acc, m, first, width):
@@ -165,10 +201,15 @@ def tile_latentattentionblock_pa_kernel(tc, x, norm_w, expand_w, q_out, k_out, g
                     stop=(g == PASSES - 1),
                 )
 
+        def q_and_k(m):
+            qk = psum.tile([P, 2, QK], F32, tag="bank")
+            project(qk[:].rearrange("p a c -> p (a c)"), m, 0, 2 * QK)
+            nc.scalar.copy(out=qk_sb[:, :, m, :], in_=qk[:])
+
         def geglu(j, m):
-            lin = mx_psum.tile([P, N_TILE], F32)
-            pre = mx_psum.tile([P, N_TILE], F32)
+            pre = psum.tile([P, N_TILE], F32, tag="bank")
             project(pre[:], m, 2 * QK + EXP + N_TILE * j, N_TILE)
+            lin = psum.tile([P, N_TILE], F32, tag="bank")
             project(lin[:], m, 2 * QK + N_TILE * j, N_TILE)
             gelu = out_pool.tile([P, N_TILE], F32)
             nc.scalar.activation(out=gelu[:], in_=pre[:], func=ACT.Gelu)
@@ -177,22 +218,28 @@ def tile_latentattentionblock_pa_kernel(tc, x, norm_w, expand_w, q_out, k_out, g
             first = N_TILE * (j % 2)
             nc.sync.dma_start(out=g_views[j // 2][:, m, first : first + N_TILE], in_=prod[:])
 
-        def q_and_k(m):
-            qk = mx_psum.tile([P, 2, QK], F32, tag="lin")
-            project(qk[:].rearrange("p a c -> p (a c)"), m, 0, 2 * QK)
-            nc.scalar.copy(out=qk_sb[:, :, m, :], in_=qk[:])
+        for m in range(AHEAD):
+            normalise(m)
+        for m in range(TOKEN_TILES):
+            if m + AHEAD < TOKEN_TILES:
+                normalise(m + AHEAD)
+            transpose_tokens(m)
+            if m >= 1:
+                quantise_tokens(m - 1)
+            for w in groups_beside(m):
+                transpose_weights(w)
+        quantise_tokens(TOKEN_TILES - 1)
+        for w in groups_after:
+            transpose_weights(w)
 
-        for c in range(TOKEN_TILES // TILES_PER_LOAD):
-            for m in range(TILES_PER_LOAD * c, TILES_PER_LOAD * (c + 1)):
-                layer_norm(m)
-            for w in group_order[4 * c : 4 * c + 4]:
-                weight_group(w)
-        weight_group(group_order[16])
-
-        for j in range(UNITS):
-            for m in range(TOKEN_TILES):
-                geglu(j, m)
+        for w in group_order[0 : 1 + GROUPS_PER_UNIT]:
+            quantise_weights(w)
         for m in range(TOKEN_TILES):
             q_and_k(m)
         nc.sync.dma_start(out=q_view, in_=qk_sb[:, 0, :, :])
         nc.sync.dma_start(out=k_view, in_=qk_sb[:, 1, :, :])
+        for j in range(UNITS):
+            for m in range(TOKEN_TILES):
+                geglu(j, m)
+                if j + 1 < UNITS and m < GROUPS_PER_UNIT:
+                    quantise_weights(group_order[1 + GROUPS_PER_UNIT * (j + 1) + m])

@@ -130,13 +130,17 @@ def tile_latentattentionblock_pa_kernel(tc, x, norm_w, expand_w, q_out, k_out, g
             nc.gpsimd.tensor_scalar(out=var_eps[:], in0=mean_var[:, 1:2], scalar1=EPS, scalar2=None, op0=ALU.add)
             rstd = small.tile([P, 1], F32)
             nc.gpsimd.tensor_tensor(out=rstd[:], in0=var_eps[:], in1=minus_half[:], op=ALU.pow)
+            minus_mean = small.tile([P, 1], F32)
+            nc.gpsimd.tensor_scalar(
+                out=minus_mean[:], in0=mean_var[:, 0:1], scalar1=-1.0, scalar2=0.0, op0=ALU.mult, op1=ALU.add
+            )
             y = y_pool.tile([P, 2, DIM // 2], F32)
             nc.gpsimd.tensor_scalar(
                 out=y[:],
                 in0=x_raw[m][:].rearrange("p (j e) -> p e j", e=2),
-                scalar1=mean_var[:, 0:1],
+                scalar1=minus_mean[:, 0:1],
                 scalar2=rstd[:, 0:1],
-                op0=ALU.subtract,
+                op0=ALU.add,
                 op1=ALU.mult,
             )
             y_tiles[m] = y

@@ -23,15 +23,18 @@ PACK = 4
 K_PASS = P * PACK
 PASSES = DIM // K_PASS
 TOKEN_TILES = TOKENS // P
+FIRST_TILES = TOKEN_TILES // 2
 GROUP_ROWS = 2 * P
 GROUPS = W_ROWS // GROUP_ROWS
 N_TILE = 512
+GROUPS_PER_PANEL = N_TILE // GROUP_ROWS
 UNITS = EXP // N_TILE
-GROUPS_PER_UNIT = 2 * N_TILE // GROUP_ROWS
-GROUPS_PER_TOKEN_TILE = (GROUPS - 1) // TOKEN_TILES
+PANELS = 2 * UNITS + 1
+TILES_PER_ROUND = 2
+ROUNDS = UNITS * FIRST_TILES // TILES_PER_ROUND
+PANELS_AHEAD = 2
 BN_CHUNK = 512
 PSUM_BANKS = 8
-AHEAD = 2
 
 FLOPS = 2 * TOKENS * DIM * W_ROWS
 
@@ -50,12 +53,13 @@ def tile_latentattentionblock_pa_kernel(tc, x, norm_w, expand_w, q_out, k_out, g
         ctx.enter_context(tc.manual_schedule())
         const = ctx.enter_context(tc.tile_pool(name="const", bufs=1))
         x_pool = ctx.enter_context(tc.tile_pool(name="x_pool", bufs=TOKEN_TILES))
-        w_pool = ctx.enter_context(tc.tile_pool(name="w_pool", bufs=8))
+        w_pool = ctx.enter_context(tc.tile_pool(name="w_pool", bufs=GROUPS))
         small = ctx.enter_context(tc.tile_pool(name="small", bufs=4))
-        y_pool = ctx.enter_context(tc.tile_pool(name="y_pool", bufs=AHEAD + 1))
+        y_pool = ctx.enter_context(tc.tile_pool(name="y_pool", bufs=FIRST_TILES))
         h_pool = ctx.enter_context(tc.tile_pool(name="h_pool", bufs=3))
-        wg_pool = ctx.enter_context(tc.tile_pool(name="wg_pool", bufs=GROUPS))
-        out_pool = ctx.enter_context(tc.tile_pool(name="out_pool", bufs=4))
+        wg_pool = ctx.enter_context(tc.tile_pool(name="wg_pool", bufs=3 * GROUPS_PER_PANEL))
+        gelu_pool = ctx.enter_context(tc.tile_pool(name="gelu_pool", bufs=3))
+        prod_pool = ctx.enter_context(tc.tile_pool(name="prod_pool", bufs=8))
         psum = ctx.enter_context(tc.psum_pool(name="psum", bufs=PSUM_BANKS))
 
         h_codes = const.tile([P, TOKEN_TILES, PASSES, P], U32, align_bytes=64)
@@ -66,14 +70,11 @@ def tile_latentattentionblock_pa_kernel(tc, x, norm_w, expand_w, q_out, k_out, g
 
         first_lin = 1
         first_pre = 1 + EXP // GROUP_ROWS
-        group_order = [0]
+        panels = []
         for j in range(UNITS):
-            group_order.extend([first_pre + 2 * j, first_pre + 2 * j + 1, first_lin + 2 * j, first_lin + 2 * j + 1])
-
-        def groups_beside(m):
-            return group_order[GROUPS_PER_TOKEN_TILE * m : GROUPS_PER_TOKEN_TILE * (m + 1)]
-
-        groups_after = group_order[GROUPS_PER_TOKEN_TILE * TOKEN_TILES :]
+            panels.append([first_pre + 2 * j, first_pre + 2 * j + 1])
+            panels.append([first_lin + 2 * j, first_lin + 2 * j + 1])
+        panels.append([0])
 
         nw_rows = const.tile([P, 2 * P], BF16)
         nc.vector.memset(nw_rows[:], 0.0)
@@ -93,23 +94,25 @@ def tile_latentattentionblock_pa_kernel(tc, x, norm_w, expand_w, q_out, k_out, g
             nc.sync.dma_start(out=x_tile[:], in_=x_view[:, m, :])
             x_raw[m] = x_tile
 
-        def load_weights(w):
-            w_chunk = w_pool.tile([P, 2, DIM], BF16)
-            nc.sync.dma_start(
-                out=w_chunk[:],
-                in_=expand_w[GROUP_ROWS * w : GROUP_ROWS * (w + 1), :].rearrange("(p t) k -> p t k", t=2),
-            )
-            w_raw[w] = w_chunk
+        def load_panel(i):
+            for w in panels[i]:
+                w_chunk = w_pool.tile([P, 2, DIM], BF16)
+                nc.sync.dma_start(
+                    out=w_chunk[:],
+                    in_=expand_w[GROUP_ROWS * w : GROUP_ROWS * (w + 1), :].rearrange("(p t) k -> p t k", t=2),
+                )
+                w_raw[w] = w_chunk
 
-        for m in range(AHEAD):
-            load_tokens(m)
-        for m in range(TOKEN_TILES):
-            for w in groups_beside(m):
-                load_weights(w)
-            if m + AHEAD < TOKEN_TILES:
-                load_tokens(m + AHEAD)
-        for w in groups_after:
-            load_weights(w)
+        load_tokens(0)
+        load_tokens(1)
+        load_panel(0)
+        load_panel(1)
+        load_tokens(2)
+        load_tokens(3)
+        for i in range(PANELS_AHEAD, PANELS):
+            load_panel(i)
+            if FIRST_TILES + i - PANELS_AHEAD < TOKEN_TILES:
+                load_tokens(FIRST_TILES + i - PANELS_AHEAD)
 
         nw_ps = psum.tile([P, P], F32, tag="bank")
         nc.tensor.transpose(nw_ps[:], nw_rows[:].bitcast(F32), ident[:])
@@ -169,29 +172,31 @@ def tile_latentattentionblock_pa_kernel(tc, x, norm_w, expand_w, q_out, k_out, g
                 in_=h_grouped_tiles[m][:].rearrange("p g r t -> p (g r t)"),
             )
 
-        def transpose_weights(w):
-            words = w_raw[w][:].bitcast(F32)
-            w_grouped = wg_pool.tile([P, PASSES, GROUP_ROWS * PACK], BF16, align_bytes=64)
-            for g in range(PASSES):
-                wt = psum.tile([P, 2, 2, P], F32, tag="bank")
-                for t in range(2):
-                    for u in range(2):
-                        first = 2 * P * g + P * u
-                        nc.tensor.transpose(wt[:, t, u, :], words[:, t, first : first + P], ident[:])
-                nc.scalar.copy(
-                    out=w_grouped[:, g, :].bitcast(F32).rearrange("p (r t u) -> p r t u", t=2, u=2),
-                    in_=wt[:].rearrange("p t u r -> p r t u"),
-                )
-            w_grouped_tiles[w] = w_grouped
+        def transpose_panel(i):
+            for w in panels[i]:
+                words = w_raw[w][:].bitcast(F32)
+                w_grouped = wg_pool.tile([P, PASSES, GROUP_ROWS * PACK], BF16, align_bytes=64)
+                for g in range(PASSES):
+                    wt = psum.tile([P, 2, 2, P], F32, tag="bank")
+                    for t in range(2):
+                        for u in range(2):
+                            first = 2 * P * g + P * u
+                            nc.tensor.transpose(wt[:, t, u, :], words[:, t, first : first + P], ident[:])
+                    nc.scalar.copy(
+                        out=w_grouped[:, g, :].bitcast(F32).rearrange("p (r t u) -> p r t u", t=2, u=2),
+                        in_=wt[:].rearrange("p t u r -> p r t u"),
+                    )
+                w_grouped_tiles[w] = w_grouped
 
-        def quantise_weights(w):
-            cols = slice(GROUP_ROWS * w, GROUP_ROWS * (w + 1))
-            for g in range(PASSES):
-                nc.vector.quantize_mx(
-                    out=w_codes[:, g, cols].bitcast(FP8X4),
-                    scales=w_scales[:, g, cols],
-                    in_=w_grouped_tiles[w][:, g, :],
-                )
+        def quantise_panel(i):
+            for w in panels[i]:
+                cols = slice(GROUP_ROWS * w, GROUP_ROWS * (w + 1))
+                for g in range(PASSES):
+                    nc.vector.quantize_mx(
+                        out=w_codes[:, g, cols].bitcast(FP8X4),
+                        scales=w_scales[:, g, cols],
+                        in_=w_grouped_tiles[w][:, g, :],
+                    )
 
         def project(acc, m, first, width):
             for g in range(PASSES):
@@ -215,35 +220,59 @@ def tile_latentattentionblock_pa_kernel(tc, x, norm_w, expand_w, q_out, k_out, g
             project(pre[:], m, 2 * QK + EXP + N_TILE * j, N_TILE)
             lin = psum.tile([P, N_TILE], F32, tag="bank")
             project(lin[:], m, 2 * QK + N_TILE * j, N_TILE)
-            gelu = out_pool.tile([P, N_TILE], F32)
+            gelu = gelu_pool.tile([P, N_TILE], F32)
             nc.scalar.activation(out=gelu[:], in_=pre[:], func=ACT.Gelu)
-            prod = out_pool.tile([P, N_TILE], F32)
+            prod = prod_pool.tile([P, N_TILE], F32)
             nc.vector.tensor_tensor(out=prod[:], in0=lin[:], in1=gelu[:], op=ALU.mult)
             first = N_TILE * (j % 2)
             nc.sync.dma_start(out=g_views[j // 2][:, m, first : first + N_TILE], in_=prod[:])
 
-        for m in range(AHEAD):
-            normalise(m)
-        for m in range(TOKEN_TILES):
-            if m + AHEAD < TOKEN_TILES:
-                normalise(m + AHEAD)
-            transpose_tokens(m)
-            if m >= 1:
-                quantise_tokens(m - 1)
-            for w in groups_beside(m):
-                transpose_weights(w)
-        quantise_tokens(TOKEN_TILES - 1)
-        for w in groups_after:
-            transpose_weights(w)
+        normalise(0)
+        normalise(1)
+        transpose_panel(0)
+        transpose_tokens(0)
+        transpose_panel(1)
+        normalise(2)
+        normalise(3)
+        quantise_tokens(0)
+        quantise_panel(0)
+        transpose_tokens(1)
+        quantise_panel(1)
+        quantise_tokens(1)
+        transpose_tokens(2)
+        transpose_tokens(3)
+        quantise_tokens(2)
+        quantise_tokens(3)
 
-        for w in group_order[0 : 1 + GROUPS_PER_UNIT]:
-            quantise_weights(w)
-        for m in range(TOKEN_TILES):
+        for r in range(ROUNDS):
+            j = r // 2
+            m = TILES_PER_ROUND * (r % 2)
+            later = r + PANELS_AHEAD
+            if later < PANELS:
+                transpose_panel(later)
+            else:
+                transpose_tokens(FIRST_TILES)
+            geglu(j, m)
+            if later < PANELS:
+                quantise_panel(later)
+            else:
+                quantise_tokens(FIRST_TILES)
+            geglu(j, m + 1)
+            if r % 2 == 0:
+                normalise(FIRST_TILES + j)
+
+        for m in range(FIRST_TILES):
             q_and_k(m)
-        nc.sync.dma_start(out=q_view, in_=qk_sb[:, 0, :, :])
-        nc.sync.dma_start(out=k_view, in_=qk_sb[:, 1, :, :])
-        for j in range(UNITS):
-            for m in range(TOKEN_TILES):
-                geglu(j, m)
-                if j + 1 < UNITS and m < GROUPS_PER_UNIT:
-                    quantise_weights(group_order[1 + GROUPS_PER_UNIT * (j + 1) + m])
+        for m in range(FIRST_TILES, TOKEN_TILES):
+            q_and_k(m)
+            if m == TOKEN_TILES - 1:
+                nc.sync.dma_start(out=q_view, in_=qk_sb[:, 0, :, :])
+                nc.sync.dma_start(out=k_view, in_=qk_sb[:, 1, :, :])
+            geglu(0, m)
+            if m + 1 < TOKEN_TILES:
+                transpose_tokens(m + 1)
+            geglu(1, m)
+            if m + 1 < TOKEN_TILES:
+                quantise_tokens(m + 1)
+            geglu(2, m)
+            geglu(3, m)

@@ -23,18 +23,16 @@ PACK = 4
 K_PASS = P * PACK
 PASSES = DIM // K_PASS
 TOKEN_TILES = TOKENS // P
-FIRST_TILES = TOKEN_TILES // 2
 GROUP_ROWS = 2 * P
 GROUPS = W_ROWS // GROUP_ROWS
 N_TILE = 512
-GROUPS_PER_PANEL = N_TILE // GROUP_ROWS
 UNITS = EXP // N_TILE
-PANELS = 2 * UNITS + 1
-TILES_PER_ROUND = 2
-ROUNDS = UNITS * FIRST_TILES // TILES_PER_ROUND
-PANELS_AHEAD = 2
+GROUPS_PER_UNIT = 2 * N_TILE // GROUP_ROWS
+GROUPS_PER_TOKEN_TILE = 2
+GROUPS_FIRST = GROUPS - GROUPS_PER_TOKEN_TILE * (TOKEN_TILES - 1)
 BN_CHUNK = 512
 PSUM_BANKS = 8
+AHEAD = 2
 
 FLOPS = 2 * TOKENS * DIM * W_ROWS
 
@@ -53,13 +51,12 @@ def tile_latentattentionblock_pa_kernel(tc, x, norm_w, expand_w, q_out, k_out, g
         ctx.enter_context(tc.manual_schedule())
         const = ctx.enter_context(tc.tile_pool(name="const", bufs=1))
         x_pool = ctx.enter_context(tc.tile_pool(name="x_pool", bufs=TOKEN_TILES))
-        w_pool = ctx.enter_context(tc.tile_pool(name="w_pool", bufs=GROUPS))
+        w_pool = ctx.enter_context(tc.tile_pool(name="w_pool", bufs=8))
         small = ctx.enter_context(tc.tile_pool(name="small", bufs=4))
-        y_pool = ctx.enter_context(tc.tile_pool(name="y_pool", bufs=FIRST_TILES))
+        y_pool = ctx.enter_context(tc.tile_pool(name="y_pool", bufs=AHEAD + 1))
         h_pool = ctx.enter_context(tc.tile_pool(name="h_pool", bufs=3))
-        wg_pool = ctx.enter_context(tc.tile_pool(name="wg_pool", bufs=3 * GROUPS_PER_PANEL))
-        gelu_pool = ctx.enter_context(tc.tile_pool(name="gelu_pool", bufs=3))
-        prod_pool = ctx.enter_context(tc.tile_pool(name="prod_pool", bufs=8))
+        wg_pool = ctx.enter_context(tc.tile_pool(name="wg_pool", bufs=GROUPS))
+        out_pool = ctx.enter_context(tc.tile_pool(name="out_pool", bufs=4))
         psum = ctx.enter_context(tc.psum_pool(name="psum", bufs=PSUM_BANKS))
 
         h_codes = const.tile([P, TOKEN_TILES, PASSES, P], U32, align_bytes=64)
@@ -70,15 +67,16 @@ def tile_latentattentionblock_pa_kernel(tc, x, norm_w, expand_w, q_out, k_out, g
 
         first_lin = 1
         first_pre = 1 + EXP // GROUP_ROWS
-        panels = []
+        group_order = [0]
         for j in range(UNITS):
-            panels.append([first_pre + 2 * j, first_pre + 2 * j + 1])
-            panels.append([first_lin + 2 * j, first_lin + 2 * j + 1])
-        panels.append([0])
+            group_order.extend([first_pre + 2 * j, first_pre + 2 * j + 1, first_lin + 2 * j, first_lin + 2 * j + 1])
+
+        def groups_behind(m):
+            first = GROUPS_FIRST + GROUPS_PER_TOKEN_TILE * m
+            return group_order[first : first + GROUPS_PER_TOKEN_TILE]
 
         nw_rows = const.tile([P, 2 * P], BF16)
         nc.vector.memset(nw_rows[:], 0.0)
-        nc.scalar.dma_start(out=nw_rows[0:PACK, :], in_=norm_w.rearrange("(c w) -> c w", w=2 * P))
         minus_half = const.tile([P, 1], F32)
         nc.vector.memset(minus_half[:], -0.5)
         ident = const.tile([P, P], F32)
@@ -94,25 +92,24 @@ def tile_latentattentionblock_pa_kernel(tc, x, norm_w, expand_w, q_out, k_out, g
             nc.sync.dma_start(out=x_tile[:], in_=x_view[:, m, :])
             x_raw[m] = x_tile
 
-        def load_panel(i):
-            for w in panels[i]:
-                w_chunk = w_pool.tile([P, 2, DIM], BF16)
-                nc.sync.dma_start(
-                    out=w_chunk[:],
-                    in_=expand_w[GROUP_ROWS * w : GROUP_ROWS * (w + 1), :].rearrange("(p t) k -> p t k", t=2),
-                )
-                w_raw[w] = w_chunk
+        def load_weights(w):
+            w_chunk = w_pool.tile([P, 2, DIM], BF16)
+            nc.sync.dma_start(
+                out=w_chunk[:],
+                in_=expand_w[GROUP_ROWS * w : GROUP_ROWS * (w + 1), :].rearrange("(p t) k -> p t k", t=2),
+            )
+            w_raw[w] = w_chunk
 
-        load_tokens(0)
-        load_tokens(1)
-        load_panel(0)
-        load_panel(1)
-        load_tokens(2)
-        load_tokens(3)
-        for i in range(PANELS_AHEAD, PANELS):
-            load_panel(i)
-            if FIRST_TILES + i - PANELS_AHEAD < TOKEN_TILES:
-                load_tokens(FIRST_TILES + i - PANELS_AHEAD)
+        for m in range(AHEAD):
+            load_tokens(m)
+        nc.sync.dma_start(out=nw_rows[0:PACK, :], in_=norm_w.rearrange("(c w) -> c w", w=2 * P))
+        for w in group_order[0:GROUPS_FIRST]:
+            load_weights(w)
+        for m in range(TOKEN_TILES):
+            if m + AHEAD < TOKEN_TILES:
+                load_tokens(m + AHEAD)
+            for w in groups_behind(m):
+                load_weights(w)
 
         nw_ps = psum.tile([P, P], F32, tag="bank")
         nc.tensor.transpose(nw_ps[:], nw_rows[:].bitcast(F32), ident[:])
@@ -172,31 +169,29 @@ def tile_latentattentionblock_pa_kernel(tc, x, norm_w, expand_w, q_out, k_out, g
                 in_=h_grouped_tiles[m][:].rearrange("p g r t -> p (g r t)"),
             )
 
-        def transpose_panel(i):
-            for w in panels[i]:
-                words = w_raw[w][:].bitcast(F32)
-                w_grouped = wg_pool.tile([P, PASSES, GROUP_ROWS * PACK], BF16, align_bytes=64)
-                for g in range(PASSES):
-                    wt = psum.tile([P, 2, 2, P], F32, tag="bank")
-                    for t in range(2):
-                        for u in range(2):
-                            first = 2 * P * g + P * u
-                            nc.tensor.transpose(wt[:, t, u, :], words[:, t, first : first + P], ident[:])
-                    nc.scalar.copy(
-                        out=w_grouped[:, g, :].bitcast(F32).rearrange("p (r t u) -> p r t u", t=2, u=2),
-                        in_=wt[:].rearrange("p t u r -> p r t u"),
-                    )
-                w_grouped_tiles[w] = w_grouped
+        def transpose_weights(w):
+            words = w_raw[w][:].bitcast(F32)
+            w_grouped = wg_pool.tile([P, PASSES, GROUP_ROWS * PACK], BF16, align_bytes=64)
+            for g in range(PASSES):
+                wt = psum.tile([P, 2, 2, P], F32, tag="bank")
+                for t in range(2):
+                    for u in range(2):
+                        first = 2 * P * g + P * u
+                        nc.tensor.transpose(wt[:, t, u, :], words[:, t, first : first + P], ident[:])
+                nc.scalar.copy(
+                    out=w_grouped[:, g, :].bitcast(F32).rearrange("p (r t u) -> p r t u", t=2, u=2),
+                    in_=wt[:].rearrange("p t u r -> p r t u"),
+                )
+            w_grouped_tiles[w] = w_grouped
 
-        def quantise_panel(i):
-            for w in panels[i]:
-                cols = slice(GROUP_ROWS * w, GROUP_ROWS * (w + 1))
-                for g in range(PASSES):
-                    nc.vector.quantize_mx(
-                        out=w_codes[:, g, cols].bitcast(FP8X4),
-                        scales=w_scales[:, g, cols],
-                        in_=w_grouped_tiles[w][:, g, :],
-                    )
+        def quantise_weights(w):
+            cols = slice(GROUP_ROWS * w, GROUP_ROWS * (w + 1))
+            for g in range(PASSES):
+                nc.vector.quantize_mx(
+                    out=w_codes[:, g, cols].bitcast(FP8X4),
+                    scales=w_scales[:, g, cols],
+                    in_=w_grouped_tiles[w][:, g, :],
+                )
 
         def project(acc, m, first, width):
             for g in range(PASSES):
@@ -220,59 +215,35 @@ def tile_latentattentionblock_pa_kernel(tc, x, norm_w, expand_w, q_out, k_out, g
             project(pre[:], m, 2 * QK + EXP + N_TILE * j, N_TILE)
             lin = psum.tile([P, N_TILE], F32, tag="bank")
             project(lin[:], m, 2 * QK + N_TILE * j, N_TILE)
-            gelu = gelu_pool.tile([P, N_TILE], F32)
+            gelu = out_pool.tile([P, N_TILE], F32)
             nc.scalar.activation(out=gelu[:], in_=pre[:], func=ACT.Gelu)
-            prod = prod_pool.tile([P, N_TILE], F32)
+            prod = out_pool.tile([P, N_TILE], F32)
             nc.vector.tensor_tensor(out=prod[:], in0=lin[:], in1=gelu[:], op=ALU.mult)
             first = N_TILE * (j % 2)
             nc.sync.dma_start(out=g_views[j // 2][:, m, first : first + N_TILE], in_=prod[:])
 
-        normalise(0)
-        normalise(1)
-        transpose_panel(0)
-        transpose_tokens(0)
-        transpose_panel(1)
-        normalise(2)
-        normalise(3)
-        quantise_tokens(0)
-        quantise_panel(0)
-        transpose_tokens(1)
-        quantise_panel(1)
-        quantise_tokens(1)
-        transpose_tokens(2)
-        transpose_tokens(3)
-        quantise_tokens(2)
-        quantise_tokens(3)
+        for m in range(AHEAD):
+            normalise(m)
+        for w in group_order[0:GROUPS_FIRST]:
+            transpose_weights(w)
+        for m in range(TOKEN_TILES):
+            if m + AHEAD < TOKEN_TILES:
+                normalise(m + AHEAD)
+            transpose_tokens(m)
+            if m >= 1:
+                quantise_tokens(m - 1)
+            if 1 <= m <= 1 + GROUPS_PER_UNIT:
+                quantise_weights(group_order[m - 1])
+            for w in groups_behind(m):
+                transpose_weights(w)
+        quantise_tokens(TOKEN_TILES - 1)
 
-        for r in range(ROUNDS):
-            j = r // 2
-            m = TILES_PER_ROUND * (r % 2)
-            later = r + PANELS_AHEAD
-            if later < PANELS:
-                transpose_panel(later)
-            else:
-                transpose_tokens(FIRST_TILES)
-            geglu(j, m)
-            if later < PANELS:
-                quantise_panel(later)
-            else:
-                quantise_tokens(FIRST_TILES)
-            geglu(j, m + 1)
-            if r % 2 == 0:
-                normalise(FIRST_TILES + j)
-
-        for m in range(FIRST_TILES):
+        for m in range(TOKEN_TILES):
             q_and_k(m)
-        for m in range(FIRST_TILES, TOKEN_TILES):
-            q_and_k(m)
-            if m == TOKEN_TILES - 1:
-                nc.sync.dma_start(out=q_view, in_=qk_sb[:, 0, :, :])
-                nc.sync.dma_start(out=k_view, in_=qk_sb[:, 1, :, :])
-            geglu(0, m)
-            if m + 1 < TOKEN_TILES:
-                transpose_tokens(m + 1)
-            geglu(1, m)
-            if m + 1 < TOKEN_TILES:
-                quantise_tokens(m + 1)
-            geglu(2, m)
-            geglu(3, m)
+        nc.sync.dma_start(out=q_view, in_=qk_sb[:, 0, :, :])
+        nc.sync.dma_start(out=k_view, in_=qk_sb[:, 1, :, :])
+        for j in range(UNITS):
+            for m in range(TOKEN_TILES):
+                geglu(j, m)
+                if j + 1 < UNITS and m < GROUPS_PER_UNIT:
+                    quantise_weights(group_order[1 + GROUPS_PER_UNIT * (j + 1) + m])

from contextlib import ExitStack

import concourse.mybir as mybir
from concourse.masks import make_identity

F32 = mybir.dt.float32
BF16 = mybir.dt.bfloat16
U32 = mybir.dt.uint32
U8 = mybir.dt.uint8
FP8X4 = mybir.dt.float8_e4m3fn_x4
ACT = mybir.ActivationFunctionType
ALU = mybir.AluOpType

P = 128
TOKENS = 1024
DIM = 1024
QK = 128
EXP = 2048
W_ROWS = 2 * QK + 2 * EXP
EPS = 1e-5

PACK = 4
K_PASS = P * PACK
PASSES = DIM // K_PASS
TOKEN_TILES = TOKENS // P
GROUP_ROWS = 2 * P
GROUPS = W_ROWS // GROUP_ROWS
N_TILE = 512
UNITS = EXP // N_TILE
GROUPS_PER_UNIT = 2 * N_TILE // GROUP_ROWS
GROUPS_PER_TOKEN_TILE = 2
GROUPS_FIRST = GROUPS - GROUPS_PER_TOKEN_TILE * (TOKEN_TILES - 1)
BN_CHUNK = 512
PSUM_BANKS = 8
AHEAD = 2

FLOPS = 2 * TOKENS * DIM * W_ROWS


def tile_latentattentionblock_pa_kernel(tc, x, norm_w, expand_w, q_out, k_out, gl_out, gv_out):
    nc = tc.nc
    x_view = x.rearrange("b (p m) k -> p (b m) k", m=TOKEN_TILES)
    q_view = q_out.rearrange("b (p m) c -> p (b m) c", m=TOKEN_TILES)
    k_view = k_out.rearrange("b (p m) c -> p (b m) c", m=TOKEN_TILES)
    g_views = [
        gl_out.rearrange("b (p m) c -> p (b m) c", m=TOKEN_TILES),
        gv_out.rearrange("b (p m) c -> p (b m) c", m=TOKEN_TILES),
    ]

    with ExitStack() as ctx:
        ctx.enter_context(tc.manual_schedule())
        const = ctx.enter_context(tc.tile_pool(name="const", bufs=1))
        x_pool = ctx.enter_context(tc.tile_pool(name="x_pool", bufs=TOKEN_TILES))
        w_pool = ctx.enter_context(tc.tile_pool(name="w_pool", bufs=8))
        small = ctx.enter_context(tc.tile_pool(name="small", bufs=4))
        y_pool = ctx.enter_context(tc.tile_pool(name="y_pool", bufs=AHEAD + 1))
        h_pool = ctx.enter_context(tc.tile_pool(name="h_pool", bufs=3))
        wg_pool = ctx.enter_context(tc.tile_pool(name="wg_pool", bufs=GROUPS))
        out_pool = ctx.enter_context(tc.tile_pool(name="out_pool", bufs=4))
        psum = ctx.enter_context(tc.psum_pool(name="psum", bufs=PSUM_BANKS))

        h_codes = const.tile([P, TOKEN_TILES, PASSES, P], U32, align_bytes=64)
        h_scales = const.tile([P, TOKEN_TILES, PASSES, P], U8, align_bytes=64)
        w_codes = const.tile([P, PASSES, W_ROWS], U32, align_bytes=64)
        w_scales = const.tile([P, PASSES, W_ROWS], U8, align_bytes=64)
        qk_sb = const.tile([P, 2, TOKEN_TILES, QK], F32)

        first_lin = 1
        first_pre = 1 + EXP // GROUP_ROWS
        group_order = [0]
        for j in range(UNITS):
            group_order.extend([first_pre + 2 * j, first_pre + 2 * j + 1, first_lin + 2 * j, first_lin + 2 * j + 1])

        def groups_behind(m):
            first = GROUPS_FIRST + GROUPS_PER_TOKEN_TILE * m
            return group_order[first : first + GROUPS_PER_TOKEN_TILE]

        nw_rows = const.tile([P, 2 * P], BF16)
        nc.vector.memset(nw_rows[:], 0.0)
        minus_half = const.tile([P, 1], F32)
        nc.vector.memset(minus_half[:], -0.5)
        ident = const.tile([P, P], F32)
        make_identity(nc, ident[:])
        table_warmer = const.tile([P, 1], F32)
        nc.scalar.activation(out=table_warmer[:], in_=minus_half[:], func=ACT.Gelu)

        x_raw = {}
        w_raw = {}

        def load_tokens(m):
            x_tile = x_pool.tile([P, DIM], BF16)
            nc.sync.dma_start(out=x_tile[:], in_=x_view[:, m, :])
            x_raw[m] = x_tile

        def load_weights(w):
            w_chunk = w_pool.tile([P, 2, DIM], BF16)
            nc.sync.dma_start(
                out=w_chunk[:],
                in_=expand_w[GROUP_ROWS * w : GROUP_ROWS * (w + 1), :].rearrange("(p t) k -> p t k", t=2),
            )
            w_raw[w] = w_chunk

        for m in range(AHEAD):
            load_tokens(m)
        nc.sync.dma_start(out=nw_rows[0:PACK, :], in_=norm_w.rearrange("(c w) -> c w", w=2 * P))
        for w in group_order[0:GROUPS_FIRST]:
            load_weights(w)
        for m in range(TOKEN_TILES):
            if m + AHEAD < TOKEN_TILES:
                load_tokens(m + AHEAD)
            for w in groups_behind(m):
                load_weights(w)

        nw_ps = psum.tile([P, P], F32, tag="bank")
        nc.tensor.transpose(nw_ps[:], nw_rows[:].bitcast(F32), ident[:])
        nw_cols = const.tile([P, PASSES * PACK], F32)
        nc.vector.tensor_copy(out=nw_cols[:], in_=nw_ps[:, 0:PACK].bitcast(BF16))

        y_tiles = {}
        h_grouped_tiles = {}
        w_grouped_tiles = {}

        def normalise(m):
            stats = small.tile([P, DIM // BN_CHUNK, 6], F32)
            for c in range(DIM // BN_CHUNK):
                nc.vector.bn_stats(out=stats[:, c, :], in_=x_raw[m][:, BN_CHUNK * c : BN_CHUNK * (c + 1)])
            mean_var = small.tile([P, 2], F32)
            nc.vector.bn_aggr(out=mean_var[:], in_=stats[:].rearrange("p c s -> p (c s)"))
            var_eps = small.tile([P, 1], F32)
            nc.gpsimd.tensor_scalar(out=var_eps[:], in0=mean_var[:, 1:2], scalar1=EPS, scalar2=None, op0=ALU.add)
            rstd = small.tile([P, 1], F32)
            nc.gpsimd.tensor_tensor(out=rstd[:], in0=var_eps[:], in1=minus_half[:], op=ALU.pow)
            minus_mean = small.tile([P, 1], F32)
            nc.gpsimd.tensor_scalar(
                out=minus_mean[:], in0=mean_var[:, 0:1], scalar1=-1.0, scalar2=0.0, op0=ALU.mult, op1=ALU.add
            )
            y = y_pool.tile([P, 2, DIM // 2], F32)
            nc.gpsimd.tensor_scalar(
                out=y[:],
                in0=x_raw[m][:].rearrange("p (j e) -> p e j", e=2),
                scalar1=minus_mean[:, 0:1],
                scalar2=rstd[:, 0:1],
                op0=ALU.add,
                op1=ALU.mult,
            )
            y_tiles[m] = y

        def transpose_tokens(m):
            y = y_tiles[m]
            h_grouped = h_pool.tile([P, PASSES, P, PACK], BF16, align_bytes=64)
            for g in range(PASSES):
                yt = psum.tile([P, PACK, P], F32, tag="bank")
                for u in range(2):
                    for e in range(2):
                        first = 2 * P * g + P * u
                        nc.tensor.transpose(yt[:, 2 * u + e, :], y[:, e, first : first + P], ident[:])
                nc.vector.tensor_tensor(
                    out=h_grouped[:, g, :, :],
                    in0=yt[:].rearrange("p t r -> p r t"),
                    in1=nw_cols[:, PACK * g : PACK * (g + 1)].unsqueeze(1).to_broadcast([P, P, PACK]),
                    op=ALU.mult,
                )
            h_grouped_tiles[m] = h_grouped

        def quantise_tokens(m):
            nc.vector.quantize_mx(
                out=h_codes[:, m, :, :].rearrange("p g r -> p (g r)").bitcast(FP8X4),
                scales=h_scales[:, m, :, :].rearrange("p g r -> p (g r)"),
                in_=h_grouped_tiles[m][:].rearrange("p g r t -> p (g r t)"),
            )

        def transpose_weights(w):
            words = w_raw[w][:].bitcast(F32)
            w_grouped = wg_pool.tile([P, PASSES, GROUP_ROWS * PACK], BF16, align_bytes=64)
            for g in range(PASSES):
                wt = psum.tile([P, 2, 2, P], F32, tag="bank")
                for t in range(2):
                    for u in range(2):
                        first = 2 * P * g + P * u
                        nc.tensor.transpose(wt[:, t, u, :], words[:, t, first : first + P], ident[:])
                nc.scalar.copy(
                    out=w_grouped[:, g, :].bitcast(F32).rearrange("p (r t u) -> p r t u", t=2, u=2),
                    in_=wt[:].rearrange("p t u r -> p r t u"),
                )
            w_grouped_tiles[w] = w_grouped

        def quantise_weights(w):
            cols = slice(GROUP_ROWS * w, GROUP_ROWS * (w + 1))
            for g in range(PASSES):
                nc.vector.quantize_mx(
                    out=w_codes[:, g, cols].bitcast(FP8X4),
                    scales=w_scales[:, g, cols],
                    in_=w_grouped_tiles[w][:, g, :],
                )

        def project(acc, m, first, width):
            for g in range(PASSES):
                nc.tensor.matmul_mx(
                    out=acc,
                    lhsT=h_codes[:, m, g, :].bitcast(FP8X4),
                    lhsT_scale=h_scales[:, m, g, :],
                    rhs=w_codes[:, g, first : first + width].bitcast(FP8X4),
                    rhs_scale=w_scales[:, g, first : first + width],
                    start=(g == 0),
                    stop=(g == PASSES - 1),
                )

        def q_and_k(m):
            qk = psum.tile([P, 2, QK], F32, tag="bank")
            project(qk[:].rearrange("p a c -> p (a c)"), m, 0, 2 * QK)
            nc.scalar.copy(out=qk_sb[:, :, m, :], in_=qk[:])

        def geglu(j, m):
            pre = psum.tile([P, N_TILE], F32, tag="bank")
            project(pre[:], m, 2 * QK + EXP + N_TILE * j, N_TILE)
            lin = psum.tile([P, N_TILE], F32, tag="bank")
            project(lin[:], m, 2 * QK + N_TILE * j, N_TILE)
            gelu = out_pool.tile([P, N_TILE], F32)
            nc.scalar.activation(out=gelu[:], in_=pre[:], func=ACT.Gelu)
            prod = out_pool.tile([P, N_TILE], F32)
            nc.vector.tensor_tensor(out=prod[:], in0=lin[:], in1=gelu[:], op=ALU.mult)
            first = N_TILE * (j % 2)
            nc.sync.dma_start(out=g_views[j // 2][:, m, first : first + N_TILE], in_=prod[:])

        for m in range(AHEAD):
            normalise(m)
        for w in group_order[0:GROUPS_FIRST]:
            transpose_weights(w)
        for m in range(TOKEN_TILES):
            if m + AHEAD < TOKEN_TILES:
                normalise(m + AHEAD)
            transpose_tokens(m)
            if m >= 1:
                quantise_tokens(m - 1)
            if 1 <= m <= 1 + GROUPS_PER_UNIT:
                quantise_weights(group_order[m - 1])
            for w in groups_behind(m):
                transpose_weights(w)
        quantise_tokens(TOKEN_TILES - 1)

        for m in range(TOKEN_TILES):
            q_and_k(m)
        nc.sync.dma_start(out=q_view, in_=qk_sb[:, 0, :, :])
        nc.sync.dma_start(out=k_view, in_=qk_sb[:, 1, :, :])
        for j in range(UNITS):
            for m in range(TOKEN_TILES):
                geglu(j, m)
                if j + 1 < UNITS and m < GROUPS_PER_UNIT:
                    quantise_weights(group_order[1 + GROUPS_PER_UNIT * (j + 1) + m])
